import numpy as np
import ml_dtypes


def mxq(x, axis, fmt="e4m3"):
    dtype, down = {"e4m3": (ml_dtypes.float8_e4m3fn, 7), "e5m2": (ml_dtypes.float8_e5m2, 14)}[fmt]
    v = np.moveaxis(np.asarray(x, np.float32).astype(ml_dtypes.bfloat16).astype(np.float64), axis, -1)
    blocks = v.reshape(v.shape[:-1] + (-1, 32))
    amax = np.abs(blocks).max(-1, keepdims=True)
    byte = np.maximum(np.where(amax > 0, np.frexp(amax)[1] - 1 + 127, 0) - down, 1)
    scale = np.exp2(byte - 127.0)
    codes = (blocks / scale).astype(np.float32).astype(dtype).astype(np.float64)
    return np.moveaxis((codes * scale).reshape(v.shape), -1, axis)


WIDE = False


def mx_kscale(k):
    if not WIDE:
        return np.ones(k)
    levels = np.array([30, -30])
    if k % 512:
        return np.exp2(np.random.permutation(np.resize(levels, k // 32))).repeat(32)
    a = np.empty((k // 512, 16))
    for p in range(k // 512):
        a[p, :8] = np.random.permutation(np.resize(levels, 8))
        for g in range(8):
            far = levels[np.abs(levels - a[p, g]) >= 10]
            a[p, g + 8] = far[np.random.randint(len(far))]
    return np.exp2(a.ravel()).repeat(32)


BF16 = ml_dtypes.bfloat16


def bf(x):
    return np.asarray(x, np.float32).astype(BF16)


def f64(x):
    return np.asarray(x).astype(np.float64)


B, S, HID, NH, NOPE, ROPE, VD, KV_RANK, SW, QB = 1, 2048, 1024, 8, 64, 128, 128, 512, 384, 128
QK = NOPE + ROPE


def rotate_half(x):
    h = x.shape[-1] // 2
    return np.concatenate([-x[..., h:], x[..., :h]], axis=-1)


def rope_tables():
    pos = np.arange(S, dtype=np.float64)
    inv = 1.0 / (10000.0 ** (np.arange(0, ROPE, 2, dtype=np.float64) / ROPE))
    ang = pos[:, None] * inv[None, :]
    ang = np.concatenate([ang, ang], axis=-1)
    return bf(np.broadcast_to(np.cos(ang)[None], (B, S, ROPE))), bf(np.broadcast_to(np.sin(ang)[None], (B, S, ROPE)))


def setup_inputs():
    s = mx_kscale(HID)
    cos, sin = rope_tables()
    return {"hidden_states": bf(np.random.standard_normal((B, S, HID)) * s), "cos": cos, "sin": sin,
            "Wq": bf(np.random.standard_normal((HID, NH * QK)) * 2.0 / np.sqrt(HID) / s[:, None]),
            "bq": bf(np.random.standard_normal(NH * QK) * 0.2)}


def reference(hidden_states, cos, sin, Wq, bq):
    q = ((mxq(f64(hidden_states), 2, "e5m2") @ mxq(f64(Wq), 0, "e4m3")) + f64(bq)).reshape(B, S, NH, QK).transpose(0, 2, 1, 3)
    q_nope, q_rope = q[..., :NOPE], q[..., NOPE:]
    c, si = f64(cos)[:, None], f64(sin)[:, None]
    q_rope = q_rope * c + rotate_half(q_rope) * si
    return np.concatenate([q_nope, q_rope], axis=-1)

@@ -1,0 +1,224 @@
+from contextlib import ExitStack
+
+import concourse.mybir as mybir
+from concourse.masks import make_identity
+
+S, HID, NH, NOPE, ROPE = 2048, 1024, 8, 64, 128
+QK = NOPE + ROPE
+HALF = ROPE // 2
+FLOPS = 2 * S * HID * NH * QK
+
+F32 = mybir.dt.float32
+BF16 = mybir.dt.bfloat16
+U32 = mybir.dt.uint32
+U8 = mybir.dt.uint8
+E4M3 = mybir.dt.float8_e4m3fn_x4
+E5M2 = mybir.dt.float8_e5m2_x4
+ALU = mybir.AluOpType
+IDENTITY = mybir.ActivationFunctionType.Identity
+
+P = 128
+PACK = 4
+K_PASS = P * PACK
+PASSES = HID // K_PASS
+ROWS = 4
+GROUP = P * ROWS
+GROUPS = S // GROUP
+PAIRS = NH // 2
+PAIR_COLS = 2 * QK
+TAB = GROUP + HALF
+
+
+def tile_gptossmlaattention_pb_kernel(tc, hidden_states, cos, sin, Wq, bq, out):
+    nc = tc.nc
+
+    with ExitStack() as ctx:
+        keep = ctx.enter_context(tc.tile_pool(name="keep", bufs=1))
+        stage = ctx.enter_context(tc.tile_pool(name="stage", bufs=3))
+        psum = ctx.enter_context(tc.psum_pool(name="psum", bufs=1))
+        ctx.enter_context(tc.manual_schedule())
+
+        ident = keep.tile([P, P], F32)
+        make_identity(nc, ident[:])
+        bias_row = keep.tile([P, NH * QK], BF16)
+        nc.vector.memset(bias_row[:].bitcast(U32), 0)
+        pick_row0 = keep.tile([P, P], BF16)
+        nc.scalar.activation(out=pick_row0[:], in_=ident[:, 0:1].broadcast_to([P, P]), func=IDENTITY)
+
+        x_raw, w_raw, tables = {}, {}, {}
+
+        def load_x(g, jj):
+            rows = hidden_states[0, g * GROUP:(g + 1) * GROUP, :].rearrange("(p j) k -> p j k", j=ROWS)
+            x_raw[g, jj] = keep.tile([P, 2, HID], BF16, name="x_raw_%d_%d" % (g, jj))
+            nc.sync.dma_start(out=x_raw[g, jj][:], in_=rows[:, 2 * jj:2 * jj + 2, :])
+
+        def load_w(pr, ps):
+            rows = Wq[ps * K_PASS:(ps + 1) * K_PASS, pr * PAIR_COLS:(pr + 1) * PAIR_COLS]
+            w_raw[pr, ps] = keep.tile([P, PACK, PAIR_COLS], BF16, name="w_raw_%d_%d" % (pr, ps))
+            nc.sync.dma_start(out=w_raw[pr, ps][:], in_=rows.rearrange("(p t) n -> p t n", t=PACK))
+
+        def load_tables(g):
+            tables[g] = keep.tile([P, 3 * TAB], BF16, name="tables_%d" % g)
+            for at, src in ((GROUP, cos), (2 * GROUP, sin)):
+                rows = src[0, g * GROUP:(g + 1) * GROUP, :].rearrange("(p j) d -> p (j d)", j=ROWS)
+                nc.sync.dma_start(out=tables[g][:, at:at + GROUP], in_=rows)
+
+        for i in range(2):
+            load_x(0, i)
+            load_w(0, i)
+        nc.sync.dma_start(out=bias_row[0:1, :], in_=bq.rearrange("(o n) -> o n", o=1))
+        for i in range(2):
+            load_w(1, i)
+        load_tables(0)
+        for n in range(1, GROUPS):
+            if n > 1:
+                for i in range(2):
+                    load_w(n, i)
+            for i in range(2):
+                load_x(n, i)
+            load_tables(n)
+
+        def negate_sin(g):
+            by_row = "p (j d) -> p j d"
+            nc.gpsimd.tensor_scalar(
+                out=tables[g][:, 0:GROUP].rearrange(by_row, j=ROWS)[:, :, 0:HALF],
+                in0=tables[g][:, 2 * GROUP:3 * GROUP].rearrange(by_row, j=ROWS)[:, :, 0:HALF],
+                scalar1=-1.0, scalar2=0.0, op0=ALU.mult, op1=ALU.add)
+
+        def factors(g, half):
+            first = GROUP if half == 0 else 0
+            two = tables[g][:, first:first + 2 * TAB].rearrange("p (m x) -> p m x", m=2)[:, :, 0:GROUP]
+            return two.rearrange("p m (j d) -> p j m d", j=ROWS)[:, :, :, 0:HALF]
+
+        grouped, codes, scales = {}, {}, {}
+
+        def transpose_x(g, ps, jj):
+            if ("x", g, ps) not in grouped:
+                grouped["x", g, ps] = stage.tile([P, GROUP * PACK], BF16, name="x_grouped", align_bytes=64)
+            words = x_raw[g, jj][:].bitcast(F32)
+            bank = psum.tile([P, 2, 2, P], F32, name="x_bank", bufs=2)
+            for jl in range(2):
+                for u in range(2):
+                    first = ps * 2 * P + u
+                    nc.tensor.transpose(bank[:, jl, u, :], words[:, jl, first:(ps + 1) * 2 * P:2], ident[:])
+            dst = grouped["x", g, ps][:].bitcast(F32)[:, jj * 4 * P:(jj + 1) * 4 * P]
+            nc.scalar.copy(out=dst.rearrange("p (j r u) -> p j r u", j=2, u=2),
+                           in_=bank[:].rearrange("p j u r -> p j r u"))
+
+        def interleave_w(pr, ps, copy):
+            grouped["w", pr, ps] = stage.tile([P, PAIR_COLS * PACK], BF16, name="w_grouped", align_bytes=64)
+            src = w_raw[pr, ps][:].rearrange("p t (h c i) -> p h c t i", h=2, i=4)
+            for first, width, at in ((0, NOPE, 0), (NOPE, ROPE, 2 * NOPE)):
+                dst = grouped["w", pr, ps][:, at * PACK:(at + 2 * width) * PACK]
+                copy(out=dst.rearrange("p (h c i t) -> p h c t i", h=2, i=4, t=PACK),
+                     in_=src[:, :, first // 4:(first + width) // 4, :, :])
+
+        def quantize(key):
+            width = grouped[key].shape[1] // PACK
+            codes[key] = keep.tile([P, width], U32, name="codes_%s_%d_%d" % key, align_bytes=64)
+            scales[key] = keep.tile([P, width], U8, name="scales_%s_%d_%d" % key, align_bytes=64)
+            nc.vector.quantize_mx(out=codes[key][:].bitcast(E5M2 if key[0] == "x" else E4M3),
+                                  scales=scales[key][:], in_=grouped[key][:])
+
+        for jj in range(2):
+            for ps in range(PASSES):
+                transpose_x(0, ps, jj)
+
+        by_head = bias_row[:].rearrange("p (h c) -> p h c", h=NH)
+        nope_bias_bank = psum.tile([P, NH, NOPE], F32, name="nope_bank", bufs=1)
+        nc.tensor.matmul(nope_bias_bank[:], lhsT=pick_row0[:], rhs=by_head[:, :, 0:NOPE], start=True, stop=True)
+        rope_bias_bank = psum.tile([P, NH], F32, name="rope_bank", bufs=2)
+        for h in range(NH):
+            nc.tensor.matmul(rope_bias_bank[:, h:h + 1], lhsT=by_head[:, h, NOPE:QK], rhs=pick_row0[:, 0:1],
+                             start=True, stop=True)
+        nope_bias = keep.tile([P, NH, NOPE], F32)
+        rope_bias = keep.tile([P, NH], F32)
+        nc.scalar.copy(out=rope_bias[:], in_=rope_bias_bank[:])
+        nc.scalar.copy(out=nope_bias[:], in_=nope_bias_bank[:])
+
+        for ps in range(PASSES):
+            interleave_w(0, ps, nc.vector.tensor_copy)
+        for ps in range(PASSES):
+            quantize(("w", 0, ps))
+            quantize(("x", 0, ps))
+        interleave_w(1, 0, nc.scalar.copy)
+        interleave_w(1, 1, nc.vector.tensor_copy)
+        for ps in range(PASSES):
+            quantize(("w", 1, ps))
+
+        units = []
+        for n in range(GROUPS):
+            units += [(g, n) for g in range(n)] + [(n, pr) for pr in range(n + 1)]
+        to_stage = [[("x", 1, ps) for ps in range(PASSES)]]
+        for n in range(2, GROUPS):
+            to_stage += [[(kind, n, ps)] for kind in ("w", "x") for ps in range(PASSES)]
+
+        staged = []
+        negated = set()
+        for step, (g, pr) in enumerate(units):
+            if g not in negated:
+                negate_sin(g)
+                negated.add(g)
+
+            rope_banks = []
+            for hl in range(2):
+                bank = psum.tile([P, GROUP], F32, name="rope_bank", bufs=2)
+                cols = slice(2 * NOPE + hl * ROPE, 2 * NOPE + (hl + 1) * ROPE)
+                for ps in range(PASSES):
+                    nc.tensor.matmul_mx(
+                        out=bank[:],
+                        lhsT=codes["w", pr, ps][:, cols].bitcast(E4M3), lhsT_scale=scales["w", pr, ps][:, cols],
+                        rhs=codes["x", g, ps][:].bitcast(E5M2), rhs_scale=scales["x", g, ps][:],
+                        start=(ps == 0), stop=(ps == PASSES - 1))
+                rope_banks.append(bank)
+            nope_bank = psum.tile([P, ROWS, 2 * NOPE], F32, name="nope_bank", bufs=1)
+            for j in range(ROWS):
+                cols = slice(j * P, (j + 1) * P)
+                for ps in range(PASSES):
+                    nc.tensor.matmul_mx(
+                        out=nope_bank[:, j, :],
+                        lhsT=codes["x", g, ps][:, cols].bitcast(E5M2), lhsT_scale=scales["x", g, ps][:, cols],
+                        rhs=codes["w", pr, ps][:, 0:2 * NOPE].bitcast(E4M3),
+                        rhs_scale=scales["w", pr, ps][:, 0:2 * NOPE],
+                        start=(ps == 0), stop=(ps == PASSES - 1))
+
+            turned = []
+            for hl in range(2):
+                h = 2 * pr + hl
+                biased = stage.tile([P, GROUP], F32, name="biased")
+                nc.scalar.activation(out=biased[:], in_=rope_banks[hl][:], func=IDENTITY, bias=rope_bias[:, h:h + 1])
+                bank = psum.tile([P, ROWS, ROPE], F32, name="turn_bank", bufs=3)
+                for j in range(ROWS):
+                    nc.tensor.transpose(bank[:, j, :], biased[:, j * P:(j + 1) * P], ident[:])
+                turned.append(bank)
+
+            to_quantize = staged
+            staged = to_stage[step] if step < len(to_stage) else []
+            for kind, n, ps in staged:
+                if kind == "x":
+                    for jj in range(2):
+                        transpose_x(n, ps, jj)
+                else:
+                    interleave_w(n, ps, nc.scalar.copy)
+
+            result = stage.tile([P, 2, ROWS, QK], F32, name="result", bufs=5)
+            nc.vector.tensor_tensor(
+                out=result[:].rearrange("p h j c -> p j h c")[:, :, :, 0:NOPE],
+                in0=nope_bank[:].rearrange("p j (h c) -> p j h c", h=2),
+                in1=nope_bias[:, 2 * pr:2 * pr + 2, :].unsqueeze(1).broadcast_to([P, ROWS, 2, NOPE]),
+                op=ALU.add)
+            for hl in range(2):
+                products = stage.tile([P, 2, ROWS, 2, HALF], F32, name="products")
+                for half in range(2):
+                    values = turned[hl][:, :, half * HALF:(half + 1) * HALF]
+                    nc.vector.tensor_tensor(
+                        out=products[:, half], in0=values.unsqueeze(2).broadcast_to([P, ROWS, 2, HALF]),
+                        in1=factors(g, half), op=ALU.mult)
+                    if hl == 0 and half == 0:
+                        for key in to_quantize:
+                            quantize(key)
+                by_row = "p j m d -> p j (m d)"
+                nc.gpsimd.tensor_tensor(out=result[:, hl, :, NOPE:QK], in0=products[:, 0].rearrange(by_row),
+                                        in1=products[:, 1].rearrange(by_row), op=ALU.add)
+                rows = out[0, 2 * pr + hl, g * GROUP:(g + 1) * GROUP, :].rearrange("(p j) c -> p (j c)", j=ROWS)
+                nc.sync.dma_start(out=rows, in_=result[:, hl].rearrange("p j c -> p (j c)"))

@@ -107,11 +107,11 @@ def tile_gptossmlaattention_pb_kernel(tc, hidden_states, cos, sin, Wq, bq, out):
 
         def interleave_w(pr, ps, copy):
             grouped["w", pr, ps] = stage.tile([P, PAIR_COLS * PACK], BF16, name="w_grouped", align_bytes=64)
-            src = w_raw[pr, ps][:].rearrange("p t (h c i) -> p h c t i", h=2, i=4)
+            src = w_raw[pr, ps][:].rearrange("p t (h c) -> p h c t", h=2)
             for first, width, at in ((0, NOPE, 0), (NOPE, ROPE, 2 * NOPE)):
                 dst = grouped["w", pr, ps][:, at * PACK:(at + 2 * width) * PACK]
-                copy(out=dst.rearrange("p (h c i t) -> p h c t i", h=2, i=4, t=PACK),
-                     in_=src[:, :, first // 4:(first + width) // 4, :, :])
+                copy(out=dst.rearrange("p (h c t) -> p h c t", h=2, t=PACK),
+                     in_=src[:, :, first:first + width, :])
 
         def quantize(key):
             width = grouped[key].shape[1] // PACK
@@ -218,7 +218,8 @@ def tile_gptossmlaattention_pb_kernel(tc, hidden_states, cos, sin, Wq, bq, out):
                         for key in to_quantize:
                             quantize(key)
                 by_row = "p j m d -> p j (m d)"
-                nc.gpsimd.tensor_tensor(out=result[:, hl, :, NOPE:QK], in0=products[:, 0].rearrange(by_row),
-                                        in1=products[:, 1].rearrange(by_row), op=ALU.add)
+                adder = nc.vector if (step == len(units) - 1 and hl == 1) else nc.gpsimd
+                adder.tensor_tensor(out=result[:, hl, :, NOPE:QK], in0=products[:, 0].rearrange(by_row),
+                                    in1=products[:, 1].rearrange(by_row), op=ALU.add)
                 rows = out[0, 2 * pr + hl, g * GROUP:(g + 1) * GROUP, :].rearrange("(p j) c -> p (j c)", j=ROWS)
                 nc.sync.dma_start(out=rows, in_=result[:, hl].rearrange("p j c -> p (j c)"))

@@ -67,16 +67,13 @@ def tile_gptossmlaattention_pb_kernel(tc, hidden_states, cos, sin, Wq, bq, out):
             load_x(0, i)
             load_w(0, i)
         nc.sync.dma_start(out=bias_row[0:1, :], in_=bq.rearrange("(o n) -> o n", o=1))
-        for i in range(2):
-            load_w(1, i)
-        load_tables(0)
         for n in range(1, GROUPS):
-            if n > 1:
-                for i in range(2):
-                    load_w(n, i)
             for i in range(2):
                 load_x(n, i)
-            load_tables(n)
+            load_tables(n - 1)
+            for i in range(2):
+                load_w(n, i)
+        load_tables(GROUPS - 1)
 
         def negate_sin(g):
             by_row = "p (j d) -> p j d"
@@ -94,7 +91,7 @@ def tile_gptossmlaattention_pb_kernel(tc, hidden_states, cos, sin, Wq, bq, out):
 
         def transpose_x(g, ps, jj):
             if ("x", g, ps) not in grouped:
-                grouped["x", g, ps] = stage.tile([P, GROUP * PACK], BF16, name="x_grouped", align_bytes=64)
+                grouped["x", g, ps] = stage.tile([P, GROUP * PACK], BF16, name="x_grouped", bufs=4, align_bytes=64)
             words = x_raw[g, jj][:].bitcast(F32)
             bank = psum.tile([P, 2, 2, P], F32, name="x_bank", bufs=2)
             for jl in range(2):
@@ -136,31 +133,32 @@ def tile_gptossmlaattention_pb_kernel(tc, hidden_states, cos, sin, Wq, bq, out):
         nc.scalar.copy(out=rope_bias[:], in_=rope_bias_bank[:])
         nc.scalar.copy(out=nope_bias[:], in_=nope_bias_bank[:])
 
+        for jj in range(2):
+            for ps in range(PASSES):
+                transpose_x(1, ps, jj)
+
         for ps in range(PASSES):
             interleave_w(0, ps, nc.vector.tensor_copy)
         for ps in range(PASSES):
             quantize(("w", 0, ps))
             quantize(("x", 0, ps))
-        interleave_w(1, 0, nc.scalar.copy)
+        interleave_w(1, 0, nc.vector.tensor_copy)
+        for ps in range(PASSES):
+            quantize(("x", 1, ps))
         interleave_w(1, 1, nc.vector.tensor_copy)
         for ps in range(PASSES):
             quantize(("w", 1, ps))
 
         units = []
         for n in range(GROUPS):
-            units += [(g, n) for g in range(n)] + [(n, pr) for pr in range(n + 1)]
-        to_stage = [[("x", 1, ps) for ps in range(PASSES)]]
-        for n in range(2, GROUPS):
-            to_stage += [[(kind, n, ps)] for kind in ("w", "x") for ps in range(PASSES)]
+            units += [(n, pr) for pr in range(n)] + [(g, n) for g in range(n + 1)]
+        to_stage = [(kind, n, ps) for n in range(2, GROUPS) for kind in ("x", "w") for ps in range(PASSES)]
 
-        staged = []
+        biased, turned, results = {}, {}, {}
         negated = set()
-        for step, (g, pr) in enumerate(units):
-            if g not in negated:
-                negate_sin(g)
-                negated.add(g)
 
-            rope_banks = []
+        def project_rope(step):
+            g, pr = units[step]
             for hl in range(2):
                 bank = psum.tile([P, GROUP], F32, name="rope_bank", bufs=2)
                 cols = slice(2 * NOPE + hl * ROPE, 2 * NOPE + (hl + 1) * ROPE)
@@ -170,56 +168,74 @@ def tile_gptossmlaattention_pb_kernel(tc, hidden_states, cos, sin, Wq, bq, out):
                         lhsT=codes["w", pr, ps][:, cols].bitcast(E4M3), lhsT_scale=scales["w", pr, ps][:, cols],
                         rhs=codes["x", g, ps][:].bitcast(E5M2), rhs_scale=scales["x", g, ps][:],
                         start=(ps == 0), stop=(ps == PASSES - 1))
-                rope_banks.append(bank)
-            nope_bank = psum.tile([P, ROWS, 2 * NOPE], F32, name="nope_bank", bufs=1)
+                h = 2 * pr + hl
+                biased[step, hl] = stage.tile([P, GROUP], F32, name="biased", bufs=4)
+                nc.scalar.activation(out=biased[step, hl][:], in_=bank[:], func=IDENTITY, bias=rope_bias[:, h:h + 1])
+
+        def project_nope(step):
+            g, pr = units[step]
+            bank = psum.tile([P, ROWS, 2 * NOPE], F32, name="nope_bank", bufs=1)
             for j in range(ROWS):
                 cols = slice(j * P, (j + 1) * P)
                 for ps in range(PASSES):
                     nc.tensor.matmul_mx(
-                        out=nope_bank[:, j, :],
+                        out=bank[:, j, :],
                         lhsT=codes["x", g, ps][:, cols].bitcast(E5M2), lhsT_scale=scales["x", g, ps][:, cols],
                         rhs=codes["w", pr, ps][:, 0:2 * NOPE].bitcast(E4M3),
                         rhs_scale=scales["w", pr, ps][:, 0:2 * NOPE],
                         start=(ps == 0), stop=(ps == PASSES - 1))
+            results[step] = stage.tile([P, 2, ROWS, QK], F32, name="result", bufs=5)
+            nc.vector.tensor_tensor(
+                out=results[step][:].rearrange("p h j c -> p j h c")[:, :, :, 0:NOPE],
+                in0=bank[:].rearrange("p j (h c) -> p j h c", h=2),
+                in1=nope_bias[:, 2 * pr:2 * pr + 2, :].unsqueeze(1).broadcast_to([P, ROWS, 2, NOPE]),
+                op=ALU.add)
 
-            turned = []
+        def turn(step):
             for hl in range(2):
-                h = 2 * pr + hl
-                biased = stage.tile([P, GROUP], F32, name="biased")
-                nc.scalar.activation(out=biased[:], in_=rope_banks[hl][:], func=IDENTITY, bias=rope_bias[:, h:h + 1])
-                bank = psum.tile([P, ROWS, ROPE], F32, name="turn_bank", bufs=3)
+                turned[step, hl] = psum.tile([P, ROWS, ROPE], F32, name="turn_bank", bufs=3)
                 for j in range(ROWS):
-                    nc.tensor.transpose(bank[:, j, :], biased[:, j * P:(j + 1) * P], ident[:])
-                turned.append(bank)
+                    nc.tensor.transpose(turned[step, hl][:, j, :], biased[step, hl][:, j * P:(j + 1) * P], ident[:])
 
-            to_quantize = staged
-            staged = to_stage[step] if step < len(to_stage) else []
-            for kind, n, ps in staged:
+        def rotate(step, hl, to_quantize):
+            g, pr = units[step]
+            if g not in negated:
+                negate_sin(g)
+                negated.add(g)
+            products = stage.tile([P, 2, ROWS, 2, HALF], F32, name="products", bufs=4)
+            for half in range(2):
+                values = turned[step, hl][:, :, half * HALF:(half + 1) * HALF]
+                nc.vector.tensor_tensor(
+                    out=products[:, half], in0=values.unsqueeze(2).broadcast_to([P, ROWS, 2, HALF]),
+                    in1=factors(g, half), op=ALU.mult)
+                if half == 0:
+                    for key in to_quantize:
+                        quantize(key)
+            by_row = "p j m d -> p j (m d)"
+            adder = nc.vector if (step == len(units) - 1 and hl == 1) else nc.gpsimd
+            adder.tensor_tensor(out=results[step][:, hl, :, NOPE:QK], in0=products[:, 0].rearrange(by_row),
+                                in1=products[:, 1].rearrange(by_row), op=ALU.add)
+            rows = out[0, 2 * pr + hl, g * GROUP:(g + 1) * GROUP, :].rearrange("(p j) c -> p (j c)", j=ROWS)
+            nc.sync.dma_start(out=rows, in_=results[step][:, hl].rearrange("p j c -> p (j c)"))
+
+        project_rope(0)
+        ready = []
+        for step in range(len(units)):
+            project_nope(step)
+            if step + 1 < len(units):
+                project_rope(step + 1)
+            if step > 0:
+                rotate(step - 1, 1, ready)
+            turn(step)
+            ready = []
+            if step < len(to_stage):
+                kind, n, ps = to_stage[step]
                 if kind == "x":
                     for jj in range(2):
                         transpose_x(n, ps, jj)
                 else:
                     interleave_w(n, ps, nc.scalar.copy)
-
-            result = stage.tile([P, 2, ROWS, QK], F32, name="result", bufs=5)
-            nc.vector.tensor_tensor(
-                out=result[:].rearrange("p h j c -> p j h c")[:, :, :, 0:NOPE],
-                in0=nope_bank[:].rearrange("p j (h c) -> p j h c", h=2),
-                in1=nope_bias[:, 2 * pr:2 * pr + 2, :].unsqueeze(1).broadcast_to([P, ROWS, 2, NOPE]),
-                op=ALU.add)
-            for hl in range(2):
-                products = stage.tile([P, 2, ROWS, 2, HALF], F32, name="products")
-                for half in range(2):
-                    values = turned[hl][:, :, half * HALF:(half + 1) * HALF]
-                    nc.vector.tensor_tensor(
-                        out=products[:, half], in0=values.unsqueeze(2).broadcast_to([P, ROWS, 2, HALF]),
-                        in1=factors(g, half), op=ALU.mult)
-                    if hl == 0 and half == 0:
-                        for key in to_quantize:
-                            quantize(key)
-                by_row = "p j m d -> p j (m d)"
-                adder = nc.vector if (step == len(units) - 1 and hl == 1) else nc.gpsimd
-                adder.tensor_tensor(out=result[:, hl, :, NOPE:QK], in0=products[:, 0].rearrange(by_row),
-                                    in1=products[:, 1].rearrange(by_row), op=ALU.add)
-                rows = out[0, 2 * pr + hl, g * GROUP:(g + 1) * GROUP, :].rearrange("(p j) c -> p (j c)", j=ROWS)
-                nc.sync.dma_start(out=rows, in_=result[:, hl].rearrange("p j c -> p (j c)"))
+                if ps == PASSES - 1:
+                    ready = [(kind, n, k) for k in range(PASSES)]
+            rotate(step, 0, [])
+        rotate(len(units) - 1, 1, [])

@@ -24,9 +24,20 @@ PASSES = HID // K_PASS
 ROWS = 4
 GROUP = P * ROWS
 GROUPS = S // GROUP
-PAIRS = NH // 2
 PAIR_COLS = 2 * QK
-TAB = GROUP + HALF
+HEAD_OPERANDS = 2
+FACTOR_STEP = GROUP + HALF
+
+ROPE_BANKS = 2
+NOPE_BANKS = 1
+TURN_BANKS = 3
+X_BANKS = 2
+
+X_GROUPED_BUFS = 4
+W_GROUPED_BUFS = 3
+BIASED_BUFS = 4
+PRODUCT_BUFS = 4
+RESULT_BUFS = 5
 
 
 def tile_gptossmlaattention_pb_kernel(tc, hidden_states, cos, sin, Wq, bq, out):
@@ -34,7 +45,7 @@ def tile_gptossmlaattention_pb_kernel(tc, hidden_states, cos, sin, Wq, bq, out):
 
     with ExitStack() as ctx:
         keep = ctx.enter_context(tc.tile_pool(name="keep", bufs=1))
-        stage = ctx.enter_context(tc.tile_pool(name="stage", bufs=3))
+        stage = ctx.enter_context(tc.tile_pool(name="stage", bufs=1))
         psum = ctx.enter_context(tc.psum_pool(name="psum", bufs=1))
         ctx.enter_context(tc.manual_schedule())
 
@@ -45,70 +56,73 @@ def tile_gptossmlaattention_pb_kernel(tc, hidden_states, cos, sin, Wq, bq, out):
         pick_row0 = keep.tile([P, P], BF16)
         nc.scalar.activation(out=pick_row0[:], in_=ident[:, 0:1].broadcast_to([P, P]), func=IDENTITY)
 
-        x_raw, w_raw, tables = {}, {}, {}
+        x_raw, w_raw, rope_tiles = {}, {}, {}
 
         def load_x(g, jj):
-            rows = hidden_states[0, g * GROUP:(g + 1) * GROUP, :].rearrange("(p j) k -> p j k", j=ROWS)
+            tokens = hidden_states[0, g * GROUP:(g + 1) * GROUP, :].rearrange("(p j) k -> p j k", j=ROWS)
             x_raw[g, jj] = keep.tile([P, 2, HID], BF16, name="x_raw_%d_%d" % (g, jj))
-            nc.sync.dma_start(out=x_raw[g, jj][:], in_=rows[:, 2 * jj:2 * jj + 2, :])
+            nc.sync.dma_start(out=x_raw[g, jj][:], in_=tokens[:, 2 * jj:2 * jj + 2, :])
 
         def load_w(pr, ps):
-            rows = Wq[ps * K_PASS:(ps + 1) * K_PASS, pr * PAIR_COLS:(pr + 1) * PAIR_COLS]
+            part = Wq[ps * K_PASS:(ps + 1) * K_PASS, pr * PAIR_COLS:(pr + 1) * PAIR_COLS]
             w_raw[pr, ps] = keep.tile([P, PACK, PAIR_COLS], BF16, name="w_raw_%d_%d" % (pr, ps))
-            nc.sync.dma_start(out=w_raw[pr, ps][:], in_=rows.rearrange("(p t) n -> p t n", t=PACK))
+            nc.sync.dma_start(out=w_raw[pr, ps][:], in_=part.rearrange("(p t) n -> p t n", t=PACK))
 
-        def load_tables(g):
-            tables[g] = keep.tile([P, 3 * TAB], BF16, name="tables_%d" % g)
+        def load_rope(g):
+            rope_tiles[g] = keep.tile([P, 3 * FACTOR_STEP], BF16, name="tables_%d" % g)
             for at, src in ((GROUP, cos), (2 * GROUP, sin)):
-                rows = src[0, g * GROUP:(g + 1) * GROUP, :].rearrange("(p j) d -> p (j d)", j=ROWS)
-                nc.sync.dma_start(out=tables[g][:, at:at + GROUP], in_=rows)
+                tokens = src[0, g * GROUP:(g + 1) * GROUP, :].rearrange("(p j) d -> p (j d)", j=ROWS)
+                nc.sync.dma_start(out=rope_tiles[g][:, at:at + GROUP], in_=tokens)
 
         for i in range(2):
             load_x(0, i)
             load_w(0, i)
         nc.sync.dma_start(out=bias_row[0:1, :], in_=bq.rearrange("(o n) -> o n", o=1))
         for n in range(1, GROUPS):
-            for i in range(2):
-                load_x(n, i)
-            load_tables(n - 1)
-            for i in range(2):
-                load_w(n, i)
-        load_tables(GROUPS - 1)
+            for jj in range(2):
+                load_x(n, jj)
+            load_rope(n - 1)
+            for ps in range(PASSES):
+                load_w(n, ps)
+        load_rope(GROUPS - 1)
 
         def negate_sin(g):
             by_row = "p (j d) -> p j d"
-            nc.gpsimd.tensor_scalar(
-                out=tables[g][:, 0:GROUP].rearrange(by_row, j=ROWS)[:, :, 0:HALF],
-                in0=tables[g][:, 2 * GROUP:3 * GROUP].rearrange(by_row, j=ROWS)[:, :, 0:HALF],
-                scalar1=-1.0, scalar2=0.0, op0=ALU.mult, op1=ALU.add)
+            nc.scalar.activation(
+                out=rope_tiles[g][:, 0:GROUP].rearrange(by_row, j=ROWS)[:, :, 0:HALF],
+                in_=rope_tiles[g][:, 2 * GROUP:3 * GROUP].rearrange(by_row, j=ROWS)[:, :, 0:HALF],
+                func=IDENTITY, scale=-1.0)
 
         def factors(g, half):
             first = GROUP if half == 0 else 0
-            two = tables[g][:, first:first + 2 * TAB].rearrange("p (m x) -> p m x", m=2)[:, :, 0:GROUP]
-            return two.rearrange("p m (j d) -> p j m d", j=ROWS)[:, :, :, 0:HALF]
+            both = rope_tiles[g][:, first:first + 2 * FACTOR_STEP].rearrange("p (m x) -> p m x", m=2)[:, :, 0:GROUP]
+            return both.rearrange("p m (j d) -> p j m d", j=ROWS)[:, :, :, 0:HALF]
 
         grouped, codes, scales = {}, {}, {}
 
         def transpose_x(g, ps, jj):
-            if ("x", g, ps) not in grouped:
-                grouped["x", g, ps] = stage.tile([P, GROUP * PACK], BF16, name="x_grouped", bufs=4, align_bytes=64)
+            if jj == 0:
+                grouped["x", g, ps] = stage.tile([P, GROUP * PACK], BF16, name="x_grouped", bufs=X_GROUPED_BUFS,
+                                                 align_bytes=64)
             words = x_raw[g, jj][:].bitcast(F32)
-            bank = psum.tile([P, 2, 2, P], F32, name="x_bank", bufs=2)
+            if g < HEAD_OPERANDS and jj == 0:
+                bank = psum.tile([P, 2, 2, P], F32, name="turn_bank", bufs=TURN_BANKS)
+            else:
+                bank = psum.tile([P, 2, 2, P], F32, name="x_bank", bufs=X_BANKS)
             for jl in range(2):
                 for u in range(2):
-                    first = ps * 2 * P + u
-                    nc.tensor.transpose(bank[:, jl, u, :], words[:, jl, first:(ps + 1) * 2 * P:2], ident[:])
+                    nc.tensor.transpose(bank[:, jl, u, :], words[:, jl, ps * 2 * P + u:(ps + 1) * 2 * P:2], ident[:])
             dst = grouped["x", g, ps][:].bitcast(F32)[:, jj * 4 * P:(jj + 1) * 4 * P]
             nc.scalar.copy(out=dst.rearrange("p (j r u) -> p j r u", j=2, u=2),
                            in_=bank[:].rearrange("p j u r -> p j r u"))
 
         def interleave_w(pr, ps, copy):
-            grouped["w", pr, ps] = stage.tile([P, PAIR_COLS * PACK], BF16, name="w_grouped", align_bytes=64)
+            grouped["w", pr, ps] = stage.tile([P, PAIR_COLS * PACK], BF16, name="w_grouped", bufs=W_GROUPED_BUFS,
+                                              align_bytes=64)
             src = w_raw[pr, ps][:].rearrange("p t (h c) -> p h c t", h=2)
             for first, width, at in ((0, NOPE, 0), (NOPE, ROPE, 2 * NOPE)):
                 dst = grouped["w", pr, ps][:, at * PACK:(at + 2 * width) * PACK]
-                copy(out=dst.rearrange("p (h c t) -> p h c t", h=2, t=PACK),
-                     in_=src[:, :, first:first + width, :])
+                copy(out=dst.rearrange("p (h c t) -> p h c t", h=2, t=PACK), in_=src[:, :, first:first + width, :])
 
         def quantize(key):
             width = grouped[key].shape[1] // PACK
@@ -122,9 +136,9 @@ def tile_gptossmlaattention_pb_kernel(tc, hidden_states, cos, sin, Wq, bq, out):
                 transpose_x(0, ps, jj)
 
         by_head = bias_row[:].rearrange("p (h c) -> p h c", h=NH)
-        nope_bias_bank = psum.tile([P, NH, NOPE], F32, name="nope_bank", bufs=1)
+        nope_bias_bank = psum.tile([P, NH, NOPE], F32, name="nope_bank", bufs=NOPE_BANKS)
         nc.tensor.matmul(nope_bias_bank[:], lhsT=pick_row0[:], rhs=by_head[:, :, 0:NOPE], start=True, stop=True)
-        rope_bias_bank = psum.tile([P, NH], F32, name="rope_bank", bufs=2)
+        rope_bias_bank = psum.tile([P, NH], F32, name="rope_bank", bufs=ROPE_BANKS)
         for h in range(NH):
             nc.tensor.matmul(rope_bias_bank[:, h:h + 1], lhsT=by_head[:, h, NOPE:QK], rhs=pick_row0[:, 0:1],
                              start=True, stop=True)
@@ -152,15 +166,15 @@ def tile_gptossmlaattention_pb_kernel(tc, hidden_states, cos, sin, Wq, bq, out):
         units = []
         for n in range(GROUPS):
             units += [(n, pr) for pr in range(n)] + [(g, n) for g in range(n + 1)]
-        to_stage = [(kind, n, ps) for n in range(2, GROUPS) for kind in ("x", "w") for ps in range(PASSES)]
+        to_stage = [(kind, n, ps) for n in range(HEAD_OPERANDS, GROUPS) for kind in ("x", "w") for ps in range(PASSES)]
+        last = len(units) - 1
 
         biased, turned, results = {}, {}, {}
-        negated = set()
 
         def project_rope(step):
             g, pr = units[step]
             for hl in range(2):
-                bank = psum.tile([P, GROUP], F32, name="rope_bank", bufs=2)
+                bank = psum.tile([P, GROUP], F32, name="rope_bank", bufs=ROPE_BANKS)
                 cols = slice(2 * NOPE + hl * ROPE, 2 * NOPE + (hl + 1) * ROPE)
                 for ps in range(PASSES):
                     nc.tensor.matmul_mx(
@@ -169,12 +183,12 @@ def tile_gptossmlaattention_pb_kernel(tc, hidden_states, cos, sin, Wq, bq, out):
                         rhs=codes["x", g, ps][:].bitcast(E5M2), rhs_scale=scales["x", g, ps][:],
                         start=(ps == 0), stop=(ps == PASSES - 1))
                 h = 2 * pr + hl
-                biased[step, hl] = stage.tile([P, GROUP], F32, name="biased", bufs=4)
+                biased[step, hl] = stage.tile([P, GROUP], F32, name="biased", bufs=BIASED_BUFS)
                 nc.scalar.activation(out=biased[step, hl][:], in_=bank[:], func=IDENTITY, bias=rope_bias[:, h:h + 1])
 
         def project_nope(step):
             g, pr = units[step]
-            bank = psum.tile([P, ROWS, 2 * NOPE], F32, name="nope_bank", bufs=1)
+            bank = psum.tile([P, ROWS, 2 * NOPE], F32, name="nope_bank", bufs=NOPE_BANKS)
             for j in range(ROWS):
                 cols = slice(j * P, (j + 1) * P)
                 for ps in range(PASSES):
@@ -184,7 +198,7 @@ def tile_gptossmlaattention_pb_kernel(tc, hidden_states, cos, sin, Wq, bq, out):
                         rhs=codes["w", pr, ps][:, 0:2 * NOPE].bitcast(E4M3),
                         rhs_scale=scales["w", pr, ps][:, 0:2 * NOPE],
                         start=(ps == 0), stop=(ps == PASSES - 1))
-            results[step] = stage.tile([P, 2, ROWS, QK], F32, name="result", bufs=5)
+            results[step] = stage.tile([P, 2, ROWS, QK], F32, name="result", bufs=RESULT_BUFS)
             nc.vector.tensor_tensor(
                 out=results[step][:].rearrange("p h j c -> p j h c")[:, :, :, 0:NOPE],
                 in0=bank[:].rearrange("p j (h c) -> p j h c", h=2),
@@ -193,16 +207,13 @@ def tile_gptossmlaattention_pb_kernel(tc, hidden_states, cos, sin, Wq, bq, out):
 
         def turn(step):
             for hl in range(2):
-                turned[step, hl] = psum.tile([P, ROWS, ROPE], F32, name="turn_bank", bufs=3)
+                turned[step, hl] = psum.tile([P, ROWS, ROPE], F32, name="turn_bank", bufs=TURN_BANKS)
                 for j in range(ROWS):
                     nc.tensor.transpose(turned[step, hl][:, j, :], biased[step, hl][:, j * P:(j + 1) * P], ident[:])
 
         def rotate(step, hl, to_quantize):
             g, pr = units[step]
-            if g not in negated:
-                negate_sin(g)
-                negated.add(g)
-            products = stage.tile([P, 2, ROWS, 2, HALF], F32, name="products", bufs=4)
+            products = stage.tile([P, 2, ROWS, 2, HALF], F32, name="products", bufs=PRODUCT_BUFS)
             for half in range(2):
                 values = turned[step, hl][:, :, half * HALF:(half + 1) * HALF]
                 nc.vector.tensor_tensor(
@@ -211,23 +222,26 @@ def tile_gptossmlaattention_pb_kernel(tc, hidden_states, cos, sin, Wq, bq, out):
                 if half == 0:
                     for key in to_quantize:
                         quantize(key)
+            adder = nc.vector if (step, hl) == (last, 1) else nc.gpsimd
             by_row = "p j m d -> p j (m d)"
-            adder = nc.vector if (step == len(units) - 1 and hl == 1) else nc.gpsimd
             adder.tensor_tensor(out=results[step][:, hl, :, NOPE:QK], in0=products[:, 0].rearrange(by_row),
                                 in1=products[:, 1].rearrange(by_row), op=ALU.add)
-            rows = out[0, 2 * pr + hl, g * GROUP:(g + 1) * GROUP, :].rearrange("(p j) c -> p (j c)", j=ROWS)
-            nc.sync.dma_start(out=rows, in_=results[step][:, hl].rearrange("p j c -> p (j c)"))
+            tokens = out[0, 2 * pr + hl, g * GROUP:(g + 1) * GROUP, :].rearrange("(p j) c -> p (j c)", j=ROWS)
+            nc.sync.dma_start(out=tokens, in_=results[step][:, hl].rearrange("p j c -> p (j c)"))
 
         project_rope(0)
-        ready = []
+        staged = []
         for step in range(len(units)):
             project_nope(step)
-            if step + 1 < len(units):
+            if step < last:
                 project_rope(step + 1)
             if step > 0:
-                rotate(step - 1, 1, ready)
+                rotate(step - 1, 1, staged)
+            g, pr = units[step]
+            if pr == 0:
+                negate_sin(g)
             turn(step)
-            ready = []
+            staged = []
             if step < len(to_stage):
                 kind, n, ps = to_stage[step]
                 if kind == "x":
@@ -236,6 +250,6 @@ def tile_gptossmlaattention_pb_kernel(tc, hidden_states, cos, sin, Wq, bq, out):
                 else:
                     interleave_w(n, ps, nc.scalar.copy)
                 if ps == PASSES - 1:
-                    ready = [(kind, n, k) for k in range(PASSES)]
+                    staged = [(kind, n, k) for k in range(PASSES)]
             rotate(step, 0, [])
-        rotate(len(units) - 1, 1, [])
+        rotate(last, 1, [])

from contextlib import ExitStack

import concourse.mybir as mybir
from concourse.masks import make_identity

S, HID, NH, NOPE, ROPE = 2048, 1024, 8, 64, 128
QK = NOPE + ROPE
HALF = ROPE // 2
FLOPS = 2 * S * HID * NH * QK

F32 = mybir.dt.float32
BF16 = mybir.dt.bfloat16
U32 = mybir.dt.uint32
U8 = mybir.dt.uint8
E4M3 = mybir.dt.float8_e4m3fn_x4
E5M2 = mybir.dt.float8_e5m2_x4
ALU = mybir.AluOpType
IDENTITY = mybir.ActivationFunctionType.Identity

P = 128
PACK = 4
K_PASS = P * PACK
PASSES = HID // K_PASS
ROWS = 4
GROUP = P * ROWS
GROUPS = S // GROUP
PAIR_COLS = 2 * QK
HEAD_OPERANDS = 2
FACTOR_STEP = GROUP + HALF

ROPE_BANKS = 2
NOPE_BANKS = 1
TURN_BANKS = 3
X_BANKS = 2

X_GROUPED_BUFS = 4
W_GROUPED_BUFS = 3
BIASED_BUFS = 4
PRODUCT_BUFS = 4
RESULT_BUFS = 5


def tile_gptossmlaattention_pb_kernel(tc, hidden_states, cos, sin, Wq, bq, out):
    nc = tc.nc

    with ExitStack() as ctx:
        keep = ctx.enter_context(tc.tile_pool(name="keep", bufs=1))
        stage = ctx.enter_context(tc.tile_pool(name="stage", bufs=1))
        psum = ctx.enter_context(tc.psum_pool(name="psum", bufs=1))
        ctx.enter_context(tc.manual_schedule())

        ident = keep.tile([P, P], F32)
        make_identity(nc, ident[:])
        bias_row = keep.tile([P, NH * QK], BF16)
        nc.vector.memset(bias_row[:].bitcast(U32), 0)
        pick_row0 = keep.tile([P, P], BF16)
        nc.scalar.activation(out=pick_row0[:], in_=ident[:, 0:1].broadcast_to([P, P]), func=IDENTITY)

        x_raw, w_raw, rope_tiles = {}, {}, {}

        def load_x(g, jj):
            tokens = hidden_states[0, g * GROUP:(g + 1) * GROUP, :].rearrange("(p j) k -> p j k", j=ROWS)
            x_raw[g, jj] = keep.tile([P, 2, HID], BF16, name="x_raw_%d_%d" % (g, jj))
            nc.sync.dma_start(out=x_raw[g, jj][:], in_=tokens[:, 2 * jj:2 * jj + 2, :])

        def load_w(pr, ps):
            part = Wq[ps * K_PASS:(ps + 1) * K_PASS, pr * PAIR_COLS:(pr + 1) * PAIR_COLS]
            w_raw[pr, ps] = keep.tile([P, PACK, PAIR_COLS], BF16, name="w_raw_%d_%d" % (pr, ps))
            nc.sync.dma_start(out=w_raw[pr, ps][:], in_=part.rearrange("(p t) n -> p t n", t=PACK))

        def load_rope(g):
            rope_tiles[g] = keep.tile([P, 3 * FACTOR_STEP], BF16, name="tables_%d" % g)
            for at, src in ((GROUP, cos), (2 * GROUP, sin)):
                tokens = src[0, g * GROUP:(g + 1) * GROUP, :].rearrange("(p j) d -> p (j d)", j=ROWS)
                nc.sync.dma_start(out=rope_tiles[g][:, at:at + GROUP], in_=tokens)

        for i in range(2):
            load_x(0, i)
            load_w(0, i)
        nc.sync.dma_start(out=bias_row[0:1, :], in_=bq.rearrange("(o n) -> o n", o=1))
        for n in range(1, GROUPS):
            for jj in range(2):
                load_x(n, jj)
            load_rope(n - 1)
            for ps in range(PASSES):
                load_w(n, ps)
        load_rope(GROUPS - 1)

        def negate_sin(g):
            by_row = "p (j d) -> p j d"
            nc.scalar.activation(
                out=rope_tiles[g][:, 0:GROUP].rearrange(by_row, j=ROWS)[:, :, 0:HALF],
                in_=rope_tiles[g][:, 2 * GROUP:3 * GROUP].rearrange(by_row, j=ROWS)[:, :, 0:HALF],
                func=IDENTITY, scale=-1.0)

        def factors(g, half):
            first = GROUP if half == 0 else 0
            both = rope_tiles[g][:, first:first + 2 * FACTOR_STEP].rearrange("p (m x) -> p m x", m=2)[:, :, 0:GROUP]
            return both.rearrange("p m (j d) -> p j m d", j=ROWS)[:, :, :, 0:HALF]

        grouped, codes, scales = {}, {}, {}

        def transpose_x(g, ps, jj):
            if jj == 0:
                grouped["x", g, ps] = stage.tile([P, GROUP * PACK], BF16, name="x_grouped", bufs=X_GROUPED_BUFS,
                                                 align_bytes=64)
            words = x_raw[g, jj][:].bitcast(F32)
            if g < HEAD_OPERANDS and jj == 0:
                bank = psum.tile([P, 2, 2, P], F32, name="turn_bank", bufs=TURN_BANKS)
            else:
                bank = psum.tile([P, 2, 2, P], F32, name="x_bank", bufs=X_BANKS)
            for jl in range(2):
                for u in range(2):
                    nc.tensor.transpose(bank[:, jl, u, :], words[:, jl, ps * 2 * P + u:(ps + 1) * 2 * P:2], ident[:])
            dst = grouped["x", g, ps][:].bitcast(F32)[:, jj * 4 * P:(jj + 1) * 4 * P]
            nc.scalar.copy(out=dst.rearrange("p (j r u) -> p j r u", j=2, u=2),
                           in_=bank[:].rearrange("p j u r -> p j r u"))

        def interleave_w(pr, ps, copy):
            grouped["w", pr, ps] = stage.tile([P, PAIR_COLS * PACK], BF16, name="w_grouped", bufs=W_GROUPED_BUFS,
                                              align_bytes=64)
            src = w_raw[pr, ps][:].rearrange("p t (h c) -> p h c t", h=2)
            for first, width, at in ((0, NOPE, 0), (NOPE, ROPE, 2 * NOPE)):
                dst = grouped["w", pr, ps][:, at * PACK:(at + 2 * width) * PACK]
                copy(out=dst.rearrange("p (h c t) -> p h c t", h=2, t=PACK), in_=src[:, :, first:first + width, :])

        def quantize(key):
            width = grouped[key].shape[1] // PACK
            codes[key] = keep.tile([P, width], U32, name="codes_%s_%d_%d" % key, align_bytes=64)
            scales[key] = keep.tile([P, width], U8, name="scales_%s_%d_%d" % key, align_bytes=64)
            nc.vector.quantize_mx(out=codes[key][:].bitcast(E5M2 if key[0] == "x" else E4M3),
                                  scales=scales[key][:], in_=grouped[key][:])

        for jj in range(2):
            for ps in range(PASSES):
                transpose_x(0, ps, jj)

        by_head = bias_row[:].rearrange("p (h c) -> p h c", h=NH)
        nope_bias_bank = psum.tile([P, NH, NOPE], F32, name="nope_bank", bufs=NOPE_BANKS)
        nc.tensor.matmul(nope_bias_bank[:], lhsT=pick_row0[:], rhs=by_head[:, :, 0:NOPE], start=True, stop=True)
        rope_bias_bank = psum.tile([P, NH], F32, name="rope_bank", bufs=ROPE_BANKS)
        for h in range(NH):
            nc.tensor.matmul(rope_bias_bank[:, h:h + 1], lhsT=by_head[:, h, NOPE:QK], rhs=pick_row0[:, 0:1],
                             start=True, stop=True)
        nope_bias = keep.tile([P, NH, NOPE], F32)
        rope_bias = keep.tile([P, NH], F32)
        nc.scalar.copy(out=rope_bias[:], in_=rope_bias_bank[:])
        nc.scalar.copy(out=nope_bias[:], in_=nope_bias_bank[:])

        for jj in range(2):
            for ps in range(PASSES):
                transpose_x(1, ps, jj)

        for ps in range(PASSES):
            interleave_w(0, ps, nc.vector.tensor_copy)
        for ps in range(PASSES):
            quantize(("w", 0, ps))
            quantize(("x", 0, ps))
        interleave_w(1, 0, nc.vector.tensor_copy)
        for ps in range(PASSES):
            quantize(("x", 1, ps))
        interleave_w(1, 1, nc.vector.tensor_copy)
        for ps in range(PASSES):
            quantize(("w", 1, ps))

        units = []
        for n in range(GROUPS):
            units += [(n, pr) for pr in range(n)] + [(g, n) for g in range(n + 1)]
        to_stage = [(kind, n, ps) for n in range(HEAD_OPERANDS, GROUPS) for kind in ("x", "w") for ps in range(PASSES)]
        last = len(units) - 1

        biased, turned, results = {}, {}, {}

        def project_rope(step):
            g, pr = units[step]
            for hl in range(2):
                bank = psum.tile([P, GROUP], F32, name="rope_bank", bufs=ROPE_BANKS)
                cols = slice(2 * NOPE + hl * ROPE, 2 * NOPE + (hl + 1) * ROPE)
                for ps in range(PASSES):
                    nc.tensor.matmul_mx(
                        out=bank[:],
                        lhsT=codes["w", pr, ps][:, cols].bitcast(E4M3), lhsT_scale=scales["w", pr, ps][:, cols],
                        rhs=codes["x", g, ps][:].bitcast(E5M2), rhs_scale=scales["x", g, ps][:],
                        start=(ps == 0), stop=(ps == PASSES - 1))
                h = 2 * pr + hl
                biased[step, hl] = stage.tile([P, GROUP], F32, name="biased", bufs=BIASED_BUFS)
                nc.scalar.activation(out=biased[step, hl][:], in_=bank[:], func=IDENTITY, bias=rope_bias[:, h:h + 1])

        def project_nope(step):
            g, pr = units[step]
            bank = psum.tile([P, ROWS, 2 * NOPE], F32, name="nope_bank", bufs=NOPE_BANKS)
            for j in range(ROWS):
                cols = slice(j * P, (j + 1) * P)
                for ps in range(PASSES):
                    nc.tensor.matmul_mx(
                        out=bank[:, j, :],
                        lhsT=codes["x", g, ps][:, cols].bitcast(E5M2), lhsT_scale=scales["x", g, ps][:, cols],
                        rhs=codes["w", pr, ps][:, 0:2 * NOPE].bitcast(E4M3),
                        rhs_scale=scales["w", pr, ps][:, 0:2 * NOPE],
                        start=(ps == 0), stop=(ps == PASSES - 1))
            results[step] = stage.tile([P, 2, ROWS, QK], F32, name="result", bufs=RESULT_BUFS)
            nc.vector.tensor_tensor(
                out=results[step][:].rearrange("p h j c -> p j h c")[:, :, :, 0:NOPE],
                in0=bank[:].rearrange("p j (h c) -> p j h c", h=2),
                in1=nope_bias[:, 2 * pr:2 * pr + 2, :].unsqueeze(1).broadcast_to([P, ROWS, 2, NOPE]),
                op=ALU.add)

        def turn(step):
            for hl in range(2):
                turned[step, hl] = psum.tile([P, ROWS, ROPE], F32, name="turn_bank", bufs=TURN_BANKS)
                for j in range(ROWS):
                    nc.tensor.transpose(turned[step, hl][:, j, :], biased[step, hl][:, j * P:(j + 1) * P], ident[:])

        def rotate(step, hl, to_quantize):
            g, pr = units[step]
            products = stage.tile([P, 2, ROWS, 2, HALF], F32, name="products", bufs=PRODUCT_BUFS)
            for half in range(2):
                values = turned[step, hl][:, :, half * HALF:(half + 1) * HALF]
                nc.vector.tensor_tensor(
                    out=products[:, half], in0=values.unsqueeze(2).broadcast_to([P, ROWS, 2, HALF]),
                    in1=factors(g, half), op=ALU.mult)
                if half == 0:
                    for key in to_quantize:
                        quantize(key)
            adder = nc.vector if (step, hl) == (last, 1) else nc.gpsimd
            by_row = "p j m d -> p j (m d)"
            adder.tensor_tensor(out=results[step][:, hl, :, NOPE:QK], in0=products[:, 0].rearrange(by_row),
                                in1=products[:, 1].rearrange(by_row), op=ALU.add)
            tokens = out[0, 2 * pr + hl, g * GROUP:(g + 1) * GROUP, :].rearrange("(p j) c -> p (j c)", j=ROWS)
            nc.sync.dma_start(out=tokens, in_=results[step][:, hl].rearrange("p j c -> p (j c)"))

        project_rope(0)
        staged = []
        for step in range(len(units)):
            project_nope(step)
            if step < last:
                project_rope(step + 1)
            if step > 0:
                rotate(step - 1, 1, staged)
            g, pr = units[step]
            if pr == 0:
                negate_sin(g)
            turn(step)
            staged = []
            if step < len(to_stage):
                kind, n, ps = to_stage[step]
                if kind == "x":
                    for jj in range(2):
                        transpose_x(n, ps, jj)
                else:
                    interleave_w(n, ps, nc.scalar.copy)
                if ps == PASSES - 1:
                    staged = [(kind, n, k) for k in range(PASSES)]
            rotate(step, 0, [])
        rotate(last, 1, [])
